import numpy as np
import ml_dtypes


def mxq(x, axis, fmt="e4m3"):
    dtype, down = {"e4m3": (ml_dtypes.float8_e4m3fn, 7), "e5m2": (ml_dtypes.float8_e5m2, 14)}[fmt]
    v = np.moveaxis(np.asarray(x, np.float32).astype(ml_dtypes.bfloat16).astype(np.float64), axis, -1)
    blocks = v.reshape(v.shape[:-1] + (-1, 32))
    amax = np.abs(blocks).max(-1, keepdims=True)
    byte = np.maximum(np.where(amax > 0, np.frexp(amax)[1] - 1 + 127, 0) - down, 1)
    scale = np.exp2(byte - 127.0)
    codes = (blocks / scale).astype(np.float32).astype(dtype).astype(np.float64)
    return np.moveaxis((codes * scale).reshape(v.shape), -1, axis)


WIDE = False


def mx_kscale(k):
    if not WIDE:
        return np.ones(k)
    levels = np.array([20, -20, 10, -10, 0])
    a = np.random.permutation(np.resize(levels, k // 512 * 4)).reshape(k // 512, 4)
    idx = np.arange(k)
    return np.exp2(a[idx // 512, idx % 128 // 32])


BF16 = ml_dtypes.bfloat16


def bf(x):
    return np.asarray(x, np.float32).astype(BF16)


def f64(x):
    return np.asarray(x).astype(np.float64)


B, D, C, SHOT, U, R = 2048, 1536, 512, 4, 2048, 8


def setup_inputs():
    s = mx_kscale(B)
    f = s / s.max()
    basis = np.random.standard_normal((R, D)) * 1.5 / np.sqrt(R * D)
    zq = np.random.standard_normal((B, R))
    zc = np.random.standard_normal((C, R))
    zu = np.random.standard_normal((U, R))
    x10 = bf(zq @ basis + np.random.standard_normal((B, D)) / np.sqrt(D))
    x2 = bf((zc @ basis)[:, None, :] + np.random.standard_normal((C, SHOT, D)) / np.sqrt(D))
    x3 = bf(zu @ basis + np.random.standard_normal((U, D)) / np.sqrt(D))
    lg = -0.5 * ((zu[:, None, :] - zc[None, :, :]) ** 2).sum(-1)
    w = np.exp(lg - lg.max(1, keepdims=True))
    w = bf(w / w.sum(1, keepdims=True))
    g = bf(np.random.standard_normal((B, C)) * np.exp2(np.random.randint(-12, 1, (B, 1))) * 16.0 * f[:, None])
    denom = SHOT + f64(w).sum(0)
    proto = (f64(x2).sum(1) + f64(w).T @ f64(x3)) / denom[:, None]
    x1 = bf(f64(x10) / f[:, None])
    return {"x1": x1.reshape(B, D, 1, 1), "x2": x2, "x3": x3, "w": w,
            "proto": np.asarray(proto, np.float32), "denom": np.asarray(denom, np.float32), "grad_out": g}


def reference(x1, x2, x3, w, proto, denom, grad_out):
    q = f64(x1).reshape(B, D)
    g = f64(grad_out)
    m = mxq(g, 0, "e5m2").T @ mxq(q, 0, "e4m3")
    gs = g.sum(0)
    dn = 2.0 * (m - gs[:, None] * f64(proto)) / f64(denom)[:, None]
    return np.repeat(dn[:, None, :], SHOT, axis=1)

@@ -1,0 +1,179 @@
+from contextlib import ExitStack
+
+import concourse.mybir as mybir
+from concourse.masks import make_identity
+
+F32 = mybir.dt.float32
+BF16 = mybir.dt.bfloat16
+U32 = mybir.dt.uint32
+U8 = mybir.dt.uint8
+E4M3_X4 = mybir.dt.float8_e4m3fn_x4
+E5M2_X4 = mybir.dt.float8_e5m2_x4
+MULT = mybir.AluOpType.mult
+ADD = mybir.AluOpType.add
+
+QUERIES, FEATURES, CLASSES, SHOT = 2048, 1536, 512, 4
+
+P = 128
+PACK = 4
+K_PASS = P * PACK
+PASSES = QUERIES // K_PASS
+N_TILE = 512
+CLASS_TILES = CLASSES // P
+FEATURE_TILES = FEATURES // N_TILE
+ROUND_CLASS_TILES = 2
+RUN = 4
+LAG = 2
+GS_COLS = 32
+
+FLOPS = 2 * QUERIES * CLASSES * FEATURES
+BYTES = 2 * QUERIES * (FEATURES + CLASSES) + 4 * CLASSES * (FEATURES + 1 + SHOT * FEATURES)
+
+
+def tile_proto_metric_semi_v_kernel(tc, x1, x2, x3, w, proto, denom, grad_out, out):
+    nc = tc.nc
+
+    q_dram = x1.rearrange("(c p j) d a b -> c p (j d a b)", p=P, j=PACK)
+    g_dram = grad_out.rearrange("(c p j) n -> c p (j n)", p=P, j=PACK)
+    proto_dram = proto.rearrange("(m p) d -> m p d", p=P)
+    denom_dram = denom.rearrange("(m p) -> m p", p=P)
+    out_dram = out.rearrange("(m p) s d -> m p s d", p=P)
+
+    with ExitStack() as ctx:
+        keep = ctx.enter_context(tc.tile_pool(name="keep", bufs=1))
+        stage = ctx.enter_context(tc.tile_pool(name="stage", bufs=6))
+        psum_acc = ctx.enter_context(
+            tc.psum_pool(name="psum_acc", bufs=ROUND_CLASS_TILES * FEATURE_TILES)
+        )
+        psum_small = ctx.enter_context(tc.psum_pool(name="psum_small", bufs=1))
+
+        g_raw = []
+        for c in range(PASSES):
+            g_raw_c = keep.tile([P, PACK, CLASSES], BF16, name="g_raw%d" % c)
+            nc.sync.dma_start(out=g_raw_c[:].rearrange("p j n -> p (j n)"), in_=g_dram[c])
+            g_raw.append(g_raw_c)
+        q_raw = []
+        for c in range(PASSES):
+            q_raw_c = keep.tile([P, PACK, FEATURES], BF16, name="q_raw%d" % c)
+            nc.sync.dma_start(out=q_raw_c[:].rearrange("p j d -> p (j d)"), in_=q_dram[c])
+            q_raw.append(q_raw_c)
+        proto_sb = []
+        for m in range(CLASS_TILES):
+            proto_m = keep.tile([P, FEATURES], F32, name="proto%d" % m)
+            nc.sync.dma_start(out=proto_m[:], in_=proto_dram[m])
+            proto_sb.append(proto_m)
+
+        identity = keep.tile([P, P], F32, name="identity")
+        make_identity(nc, identity[:])
+        denom_rows = keep.tile([P, P], F32, name="denom_rows")
+        nc.vector.memset(denom_rows[:], 0.0)
+        nc.scalar.dma_start(out=denom_rows[0:CLASS_TILES, :], in_=denom_dram)
+        ones = keep.tile([P, GS_COLS], BF16, name="ones")
+        nc.vector.memset(ones[:], 1.0)
+
+        g_codes = keep.tile([P, PASSES, CLASSES], U32, name="g_codes", align_bytes=64)
+        g_scales = keep.tile([P, PASSES, CLASSES], U8, name="g_scales", align_bytes=64)
+        q_codes = keep.tile([P, PASSES, FEATURES], U32, name="q_codes", align_bytes=64)
+        q_scales = keep.tile([P, PASSES, FEATURES], U8, name="q_scales", align_bytes=64)
+
+        pieces = []
+        for c in range(PASSES):
+            pieces.append((g_raw[c][:, :, :], g_codes[:, c, :], g_scales[:, c, :], E5M2_X4))
+        for c in range(PASSES):
+            for n in range(FEATURE_TILES):
+                cols = slice(n * N_TILE, (n + 1) * N_TILE)
+                pieces.append(
+                    (q_raw[c][:, :, cols], q_codes[:, c, cols], q_scales[:, c, cols], E4M3_X4)
+                )
+
+        def regroup(index):
+            source = pieces[index][0]
+            grouped = stage.tile([P, N_TILE, PACK], BF16, name="grouped", align_bytes=64)
+            copy = nc.vector.tensor_copy if index % 2 == 0 else nc.scalar.copy
+            copy(
+                out=grouped[:].rearrange("p (r i) j -> p r j i", i=RUN),
+                in_=source.rearrange("p j (r i) -> p r j i", i=RUN),
+            )
+            return grouped
+
+        def quantise(index, grouped):
+            words, scale_bytes, packed = pieces[index][1:]
+            nc.vector.quantize_mx(
+                out=words.bitcast(packed),
+                scales=scale_bytes,
+                in_=grouped[:].rearrange("p col j -> p (col j)"),
+            )
+
+        grouped_tiles = []
+        for index in range(len(pieces) + LAG):
+            if index < len(pieces):
+                grouped_tiles.append(regroup(index))
+            if index >= LAG:
+                quantise(index - LAG, grouped_tiles[index - LAG])
+
+        denom_ps = psum_small.tile([P, P], F32, name="denom_ps")
+        nc.tensor.transpose(denom_ps[:], denom_rows[:], identity[:])
+        gs_ps = psum_small.tile([P, CLASS_TILES, GS_COLS], F32, name="gs_ps")
+        for m in range(CLASS_TILES):
+            for c in range(PASSES):
+                for j in range(PACK):
+                    nc.tensor.matmul(
+                        out=gs_ps[:, m, :],
+                        lhsT=g_raw[c][:, j, m * P : (m + 1) * P],
+                        rhs=ones[:],
+                        start=(c == 0 and j == 0),
+                        stop=(c == PASSES - 1 and j == PACK - 1),
+                    )
+        m_factor = keep.tile([P, CLASS_TILES], F32, name="m_factor")
+        nc.vector.reciprocal(out=m_factor[:], in_=denom_ps[:, 0:CLASS_TILES])
+        nc.vector.tensor_scalar_mul(out=m_factor[:], in0=m_factor[:], scalar1=2.0)
+        proto_factor = keep.tile([P, CLASS_TILES], F32, name="proto_factor")
+        nc.vector.scalar_tensor_tensor(
+            out=proto_factor[:],
+            in0=gs_ps[:, :, 0],
+            scalar=-1.0,
+            in1=m_factor[:],
+            op0=MULT,
+            op1=MULT,
+        )
+
+        for first in range(0, CLASS_TILES, ROUND_CLASS_TILES):
+            class_tiles = range(first, first + ROUND_CLASS_TILES)
+            acc = {}
+            for m in class_tiles:
+                for n in range(FEATURE_TILES):
+                    acc[m, n] = psum_acc.tile([P, N_TILE], F32, name="acc_%d_%d" % (m, n), tag="acc")
+            for c in range(PASSES):
+                for m in class_tiles:
+                    for n in range(FEATURE_TILES):
+                        nc.tensor.matmul_mx(
+                            out=acc[m, n][:],
+                            lhsT=g_codes[:, c, m * P : (m + 1) * P].bitcast(E5M2_X4),
+                            lhsT_scale=g_scales[:, c, m * P : (m + 1) * P],
+                            rhs=q_codes[:, c, n * N_TILE : (n + 1) * N_TILE].bitcast(E4M3_X4),
+                            rhs_scale=q_scales[:, c, n * N_TILE : (n + 1) * N_TILE],
+                            start=(c == 0),
+                            stop=(c == PASSES - 1),
+                        )
+            for m in class_tiles:
+                nc.scalar.activation(
+                    out=proto_sb[m][:],
+                    in_=proto_sb[m][:],
+                    func=mybir.ActivationFunctionType.Copy,
+                    scale=proto_factor[:, m : m + 1],
+                )
+                result = keep.tile([P, FEATURES], F32, name="result%d" % m)
+                for n in range(FEATURE_TILES):
+                    cols = slice(n * N_TILE, (n + 1) * N_TILE)
+                    nc.vector.scalar_tensor_tensor(
+                        out=result[:, cols],
+                        in0=acc[m, n][:],
+                        scalar=m_factor[:, m : m + 1],
+                        in1=proto_sb[m][:, cols],
+                        op0=MULT,
+                        op1=ADD,
+                    )
+                nc.sync.dma_start(
+                    out=out_dram[m],
+                    in_=result[:].unsqueeze(1).to_broadcast([P, SHOT, FEATURES]),
+                )

@@ -21,9 +21,8 @@ PASSES = QUERIES // K_PASS
 N_TILE = 512
 CLASS_TILES = CLASSES // P
 FEATURE_TILES = FEATURES // N_TILE
-ROUND_CLASS_TILES = 2
+EARLY_CLASS_TILES = 2
 RUN = 4
-LAG = 2
 GS_COLS = 32
 
 FLOPS = 2 * QUERIES * CLASSES * FEATURES
@@ -41,9 +40,9 @@ def tile_proto_metric_semi_v_kernel(tc, x1, x2, x3, w, proto, denom, grad_out, o
 
     with ExitStack() as ctx:
         keep = ctx.enter_context(tc.tile_pool(name="keep", bufs=1))
-        stage = ctx.enter_context(tc.tile_pool(name="stage", bufs=6))
+        stage = ctx.enter_context(tc.tile_pool(name="stage", bufs=4))
         psum_acc = ctx.enter_context(
-            tc.psum_pool(name="psum_acc", bufs=ROUND_CLASS_TILES * FEATURE_TILES)
+            tc.psum_pool(name="psum_acc", bufs=EARLY_CLASS_TILES * FEATURE_TILES)
         )
         psum_small = ctx.enter_context(tc.psum_pool(name="psum_small", bufs=1))
 
@@ -89,30 +88,71 @@ def tile_proto_metric_semi_v_kernel(tc, x1, x2, x3, w, proto, denom, grad_out, o
         def regroup(index):
             source = pieces[index][0]
             grouped = stage.tile([P, N_TILE, PACK], BF16, name="grouped", align_bytes=64)
-            copy = nc.vector.tensor_copy if index % 2 == 0 else nc.scalar.copy
+            copy = nc.vector.tensor_copy if index % 2 == 1 else nc.scalar.copy
             copy(
                 out=grouped[:].rearrange("p (r i) j -> p r j i", i=RUN),
                 in_=source.rearrange("p j (r i) -> p r j i", i=RUN),
             )
             return grouped
 
-        def quantise(index, grouped):
+        regrouped = [regroup(0)]
+
+        def quantise(index):
+            if index + 1 < len(pieces):
+                regrouped.append(regroup(index + 1))
             words, scale_bytes, packed = pieces[index][1:]
             nc.vector.quantize_mx(
                 out=words.bitcast(packed),
                 scales=scale_bytes,
-                in_=grouped[:].rearrange("p col j -> p (col j)"),
+                in_=regrouped[index][:].rearrange("p col j -> p (col j)"),
             )
 
-        grouped_tiles = []
-        for index in range(len(pieces) + LAG):
-            if index < len(pieces):
-                grouped_tiles.append(regroup(index))
-            if index >= LAG:
-                quantise(index - LAG, grouped_tiles[index - LAG])
+        acc = {}
 
-        denom_ps = psum_small.tile([P, P], F32, name="denom_ps")
-        nc.tensor.transpose(denom_ps[:], denom_rows[:], identity[:])
+        def open_bank(m, n):
+            acc[m, n] = psum_acc.tile([P, N_TILE], F32, name="acc_%d_%d" % (m, n), tag="acc")
+
+        def multiply(c, m, n):
+            nc.tensor.matmul_mx(
+                out=acc[m, n][:],
+                lhsT=g_codes[:, c, m * P : (m + 1) * P].bitcast(E5M2_X4),
+                lhsT_scale=g_scales[:, c, m * P : (m + 1) * P],
+                rhs=q_codes[:, c, n * N_TILE : (n + 1) * N_TILE].bitcast(E4M3_X4),
+                rhs_scale=q_scales[:, c, n * N_TILE : (n + 1) * N_TILE],
+                start=(c == 0),
+                stop=(c == PASSES - 1),
+            )
+
+        result = []
+        for m in range(CLASS_TILES):
+            result.append(keep.tile([P, FEATURES], F32, name="result%d" % m))
+
+        def finish(m, n):
+            cols = slice(n * N_TILE, (n + 1) * N_TILE)
+            difference = stage.tile([P, N_TILE], F32, name="difference")
+            nc.vector.scalar_tensor_tensor(
+                out=difference[:],
+                in0=proto_sb[m][:, cols],
+                scalar=minus_gs[:, m : m + 1],
+                in1=acc[m, n][:],
+                op0=MULT,
+                op1=ADD,
+            )
+            nc.scalar.activation(
+                out=result[m][:, cols],
+                in_=difference[:],
+                func=mybir.ActivationFunctionType.Copy,
+                scale=two_over_denom[:, m : m + 1],
+            )
+
+        def store(m, cols, width):
+            nc.sync.dma_start(
+                out=out_dram[m][:, :, cols],
+                in_=result[m][:, cols].unsqueeze(1).to_broadcast([P, SHOT, width]),
+            )
+
+        for c in range(PASSES):
+            quantise(c)
         gs_ps = psum_small.tile([P, CLASS_TILES, GS_COLS], F32, name="gs_ps")
         for m in range(CLASS_TILES):
             for c in range(PASSES):
@@ -124,56 +164,35 @@ def tile_proto_metric_semi_v_kernel(tc, x1, x2, x3, w, proto, denom, grad_out, o
                         start=(c == 0 and j == 0),
                         stop=(c == PASSES - 1 and j == PACK - 1),
                     )
-        m_factor = keep.tile([P, CLASS_TILES], F32, name="m_factor")
-        nc.vector.reciprocal(out=m_factor[:], in_=denom_ps[:, 0:CLASS_TILES])
-        nc.vector.tensor_scalar_mul(out=m_factor[:], in0=m_factor[:], scalar1=2.0)
-        proto_factor = keep.tile([P, CLASS_TILES], F32, name="proto_factor")
-        nc.vector.scalar_tensor_tensor(
-            out=proto_factor[:],
-            in0=gs_ps[:, :, 0],
-            scalar=-1.0,
-            in1=m_factor[:],
-            op0=MULT,
-            op1=MULT,
-        )
+        minus_gs = keep.tile([P, CLASS_TILES], F32, name="minus_gs")
+        nc.vector.tensor_scalar_mul(out=minus_gs[:], in0=gs_ps[:, :, 0], scalar1=-1.0)
+        denom_ps = psum_small.tile([P, P], F32, name="denom_ps")
+        nc.tensor.transpose(denom_ps[:], denom_rows[:], identity[:])
+        one_over_denom = keep.tile([P, CLASS_TILES], F32, name="one_over_denom")
+        nc.vector.reciprocal(out=one_over_denom[:], in_=denom_ps[:, 0:CLASS_TILES])
+        two_over_denom = keep.tile([P, CLASS_TILES], F32, name="two_over_denom")
+        nc.vector.tensor_scalar_mul(out=two_over_denom[:], in0=one_over_denom[:], scalar1=2.0)
 
-        for first in range(0, CLASS_TILES, ROUND_CLASS_TILES):
-            class_tiles = range(first, first + ROUND_CLASS_TILES)
-            acc = {}
-            for m in class_tiles:
-                for n in range(FEATURE_TILES):
-                    acc[m, n] = psum_acc.tile([P, N_TILE], F32, name="acc_%d_%d" % (m, n), tag="acc")
-            for c in range(PASSES):
-                for m in class_tiles:
-                    for n in range(FEATURE_TILES):
-                        nc.tensor.matmul_mx(
-                            out=acc[m, n][:],
-                            lhsT=g_codes[:, c, m * P : (m + 1) * P].bitcast(E5M2_X4),
-                            lhsT_scale=g_scales[:, c, m * P : (m + 1) * P],
-                            rhs=q_codes[:, c, n * N_TILE : (n + 1) * N_TILE].bitcast(E4M3_X4),
-                            rhs_scale=q_scales[:, c, n * N_TILE : (n + 1) * N_TILE],
-                            start=(c == 0),
-                            stop=(c == PASSES - 1),
-                        )
-            for m in class_tiles:
-                nc.scalar.activation(
-                    out=proto_sb[m][:],
-                    in_=proto_sb[m][:],
-                    func=mybir.ActivationFunctionType.Copy,
-                    scale=proto_factor[:, m : m + 1],
-                )
-                result = keep.tile([P, FEATURES], F32, name="result%d" % m)
-                for n in range(FEATURE_TILES):
-                    cols = slice(n * N_TILE, (n + 1) * N_TILE)
-                    nc.vector.scalar_tensor_tensor(
-                        out=result[:, cols],
-                        in0=acc[m, n][:],
-                        scalar=m_factor[:, m : m + 1],
-                        in1=proto_sb[m][:, cols],
-                        op0=MULT,
-                        op1=ADD,
-                    )
-                nc.sync.dma_start(
-                    out=out_dram[m],
-                    in_=result[:].unsqueeze(1).to_broadcast([P, SHOT, FEATURES]),
-                )
+        for m in range(EARLY_CLASS_TILES):
+            for n in range(FEATURE_TILES):
+                open_bank(m, n)
+        for c in range(PASSES):
+            for n in range(FEATURE_TILES):
+                quantise(PASSES + c * FEATURE_TILES + n)
+                for m in range(EARLY_CLASS_TILES):
+                    multiply(c, m, n)
+                if c == PASSES - 1:
+                    finish(0, n)
+                    store(0, slice(n * N_TILE, (n + 1) * N_TILE), N_TILE)
+        for m in range(1, EARLY_CLASS_TILES):
+            for n in range(FEATURE_TILES):
+                finish(m, n)
+            store(m, slice(0, FEATURES), FEATURES)
+
+        for m in range(EARLY_CLASS_TILES, CLASS_TILES):
+            for n in range(FEATURE_TILES):
+                open_bank(m, n)
+                for c in range(PASSES):
+                    multiply(c, m, n)
+                finish(m, n)
+            store(m, slice(0, FEATURES), FEATURES)

@@ -88,7 +88,8 @@ def tile_proto_metric_semi_v_kernel(tc, x1, x2, x3, w, proto, denom, grad_out, o
         def regroup(index):
             source = pieces[index][0]
             grouped = stage.tile([P, N_TILE, PACK], BF16, name="grouped", align_bytes=64)
-            copy = nc.vector.tensor_copy if index % 2 == 1 else nc.scalar.copy
+            on_vector = index % 2 == 1 and index != len(pieces) - 1
+            copy = nc.vector.tensor_copy if on_vector else nc.scalar.copy
             copy(
                 out=grouped[:].rearrange("p (r i) j -> p r j i", i=RUN),
                 in_=source.rearrange("p j (r i) -> p r j i", i=RUN),
@@ -127,22 +128,31 @@ def tile_proto_metric_semi_v_kernel(tc, x1, x2, x3, w, proto, denom, grad_out, o
         for m in range(CLASS_TILES):
             result.append(keep.tile([P, FEATURES], F32, name="result%d" % m))
 
+        def scale_proto(m, n):
+            cols = slice(n * N_TILE, (n + 1) * N_TILE)
+            if n == 0:
+                nc.vector.tensor_scalar_mul(
+                    out=proto_sb[m][:, cols],
+                    in0=proto_sb[m][:, cols],
+                    scalar1=proto_factor[:, m : m + 1],
+                )
+            else:
+                nc.scalar.activation(
+                    out=proto_sb[m][:, cols],
+                    in_=proto_sb[m][:, cols],
+                    func=mybir.ActivationFunctionType.Copy,
+                    scale=proto_factor[:, m : m + 1],
+                )
+
         def finish(m, n):
             cols = slice(n * N_TILE, (n + 1) * N_TILE)
-            difference = stage.tile([P, N_TILE], F32, name="difference")
             nc.vector.scalar_tensor_tensor(
-                out=difference[:],
-                in0=proto_sb[m][:, cols],
-                scalar=minus_gs[:, m : m + 1],
-                in1=acc[m, n][:],
+                out=result[m][:, cols],
+                in0=acc[m, n][:],
+                scalar=two_over_denom[:, m : m + 1],
+                in1=proto_sb[m][:, cols],
                 op0=MULT,
                 op1=ADD,
-            )
-            nc.scalar.activation(
-                out=result[m][:, cols],
-                in_=difference[:],
-                func=mybir.ActivationFunctionType.Copy,
-                scale=two_over_denom[:, m : m + 1],
             )
 
         def store(m, cols, width):
@@ -164,35 +174,53 @@ def tile_proto_metric_semi_v_kernel(tc, x1, x2, x3, w, proto, denom, grad_out, o
                         start=(c == 0 and j == 0),
                         stop=(c == PASSES - 1 and j == PACK - 1),
                     )
-        minus_gs = keep.tile([P, CLASS_TILES], F32, name="minus_gs")
-        nc.vector.tensor_scalar_mul(out=minus_gs[:], in0=gs_ps[:, :, 0], scalar1=-1.0)
         denom_ps = psum_small.tile([P, P], F32, name="denom_ps")
         nc.tensor.transpose(denom_ps[:], denom_rows[:], identity[:])
-        one_over_denom = keep.tile([P, CLASS_TILES], F32, name="one_over_denom")
-        nc.vector.reciprocal(out=one_over_denom[:], in_=denom_ps[:, 0:CLASS_TILES])
-        two_over_denom = keep.tile([P, CLASS_TILES], F32, name="two_over_denom")
-        nc.vector.tensor_scalar_mul(out=two_over_denom[:], in0=one_over_denom[:], scalar1=2.0)
+
+        def quantise_and_multiply(c, n):
+            quantise(PASSES + c * FEATURE_TILES + n)
+            for m in range(EARLY_CLASS_TILES):
+                multiply(c, m, n)
 
         for m in range(EARLY_CLASS_TILES):
             for n in range(FEATURE_TILES):
                 open_bank(m, n)
-        for c in range(PASSES):
+        for c in range(PASSES - 1):
             for n in range(FEATURE_TILES):
-                quantise(PASSES + c * FEATURE_TILES + n)
-                for m in range(EARLY_CLASS_TILES):
-                    multiply(c, m, n)
-                if c == PASSES - 1:
-                    finish(0, n)
-                    store(0, slice(n * N_TILE, (n + 1) * N_TILE), N_TILE)
-        for m in range(1, EARLY_CLASS_TILES):
-            for n in range(FEATURE_TILES):
+                quantise_and_multiply(c, n)
+
+        one_over_denom = keep.tile([P, CLASS_TILES], F32, name="one_over_denom")
+        nc.vector.reciprocal(out=one_over_denom[:], in_=denom_ps[:, 0:CLASS_TILES])
+        two_over_denom = keep.tile([P, CLASS_TILES], F32, name="two_over_denom")
+        nc.vector.tensor_scalar_mul(out=two_over_denom[:], in0=one_over_denom[:], scalar1=2.0)
+        proto_factor = keep.tile([P, CLASS_TILES], F32, name="proto_factor")
+        nc.vector.scalar_tensor_tensor(
+            out=proto_factor[:],
+            in0=gs_ps[:, :, 0],
+            scalar=-1.0,
+            in1=two_over_denom[:],
+            op0=MULT,
+            op1=MULT,
+        )
+
+        quantise_and_multiply(PASSES - 1, 0)
+        for m in range(EARLY_CLASS_TILES):
+            scale_proto(m, 0)
+            finish(m, 0)
+            store(m, slice(0, N_TILE), N_TILE)
+        for n in range(1, FEATURE_TILES):
+            quantise_and_multiply(PASSES - 1, n)
+        for m in range(EARLY_CLASS_TILES):
+            for n in range(1, FEATURE_TILES):
+                scale_proto(m, n)
                 finish(m, n)
-            store(m, slice(0, FEATURES), FEATURES)
+            store(m, slice(N_TILE, FEATURES), FEATURES - N_TILE)
 
         for m in range(EARLY_CLASS_TILES, CLASS_TILES):
             for n in range(FEATURE_TILES):
                 open_bank(m, n)
                 for c in range(PASSES):
                     multiply(c, m, n)
+                scale_proto(m, n)
                 finish(m, n)
             store(m, slice(0, FEATURES), FEATURES)

@@ -41,6 +41,8 @@ def tile_proto_metric_semi_v_kernel(tc, x1, x2, x3, w, proto, denom, grad_out, o
     with ExitStack() as ctx:
         keep = ctx.enter_context(tc.tile_pool(name="keep", bufs=1))
         stage = ctx.enter_context(tc.tile_pool(name="stage", bufs=4))
+        big = ctx.enter_context(tc.tile_pool(name="big", bufs=PASSES))
+        diffs = ctx.enter_context(tc.tile_pool(name="diffs", bufs=3))
         psum_acc = ctx.enter_context(
             tc.psum_pool(name="psum_acc", bufs=EARLY_CLASS_TILES * FEATURE_TILES)
         )
@@ -53,7 +55,7 @@ def tile_proto_metric_semi_v_kernel(tc, x1, x2, x3, w, proto, denom, grad_out, o
             g_raw.append(g_raw_c)
         q_raw = []
         for c in range(PASSES):
-            q_raw_c = keep.tile([P, PACK, FEATURES], BF16, name="q_raw%d" % c)
+            q_raw_c = big.tile([P, PACK, FEATURES], BF16, name="q_raw%d" % c, tag="big")
             nc.sync.dma_start(out=q_raw_c[:].rearrange("p j d -> p (j d)"), in_=q_dram[c])
             q_raw.append(q_raw_c)
         proto_sb = []
@@ -124,9 +126,8 @@ def tile_proto_metric_semi_v_kernel(tc, x1, x2, x3, w, proto, denom, grad_out, o
                 stop=(c == PASSES - 1),
             )
 
-        result = []
-        for m in range(CLASS_TILES):
-            result.append(keep.tile([P, FEATURES], F32, name="result%d" % m))
+        result = [keep.tile([P, FEATURES], F32, name="result0")]
+        repeated = {}
 
         def scale_proto(m, n):
             cols = slice(n * N_TILE, (n + 1) * N_TILE)
@@ -153,6 +154,37 @@ def tile_proto_metric_semi_v_kernel(tc, x1, x2, x3, w, proto, denom, grad_out, o
                 in1=proto_sb[m][:, cols],
                 op0=MULT,
                 op1=ADD,
+            )
+
+        def finish_repeated(m, n):
+            cols = slice(n * N_TILE, (n + 1) * N_TILE)
+            diff = diffs.tile([P, N_TILE], F32, name="diff")
+            nc.vector.scalar_tensor_tensor(
+                out=diff[:],
+                in0=proto_sb[m][:, cols],
+                scalar=minus_gs[:, m : m + 1],
+                in1=acc[m, n][:],
+                op0=MULT,
+                op1=ADD,
+            )
+            half = SHOT // 2
+            twice = diff[:].unsqueeze(1).to_broadcast([P, half, N_TILE])
+            nc.scalar.activation(
+                out=repeated[m][:, 0:half, cols],
+                in_=twice,
+                func=mybir.ActivationFunctionType.Copy,
+                scale=two_over_denom[:, m : m + 1],
+            )
+            nc.vector.tensor_scalar_mul(
+                out=repeated[m][:, half:SHOT, cols],
+                in0=twice,
+                scalar1=two_over_denom[:, m : m + 1],
+            )
+
+        def store_repeated(m):
+            nc.sync.dma_start(
+                out=out_dram[m].rearrange("p s d -> p (s d)"),
+                in_=repeated[m][:].rearrange("p s d -> p (s d)"),
             )
 
         def store(m, cols, width):
@@ -193,34 +225,32 @@ def tile_proto_metric_semi_v_kernel(tc, x1, x2, x3, w, proto, denom, grad_out, o
         nc.vector.reciprocal(out=one_over_denom[:], in_=denom_ps[:, 0:CLASS_TILES])
         two_over_denom = keep.tile([P, CLASS_TILES], F32, name="two_over_denom")
         nc.vector.tensor_scalar_mul(out=two_over_denom[:], in0=one_over_denom[:], scalar1=2.0)
+        minus_gs = keep.tile([P, CLASS_TILES], F32, name="minus_gs")
+        nc.vector.tensor_scalar_mul(out=minus_gs[:], in0=gs_ps[:, :, 0], scalar1=-1.0)
         proto_factor = keep.tile([P, CLASS_TILES], F32, name="proto_factor")
-        nc.vector.scalar_tensor_tensor(
-            out=proto_factor[:],
-            in0=gs_ps[:, :, 0],
-            scalar=-1.0,
-            in1=two_over_denom[:],
-            op0=MULT,
-            op1=MULT,
-        )
+        nc.vector.tensor_mul(out=proto_factor[:], in0=minus_gs[:], in1=two_over_denom[:])
 
         quantise_and_multiply(PASSES - 1, 0)
-        for m in range(EARLY_CLASS_TILES):
-            scale_proto(m, 0)
-            finish(m, 0)
-            store(m, slice(0, N_TILE), N_TILE)
+        scale_proto(0, 0)
+        finish(0, 0)
+        store(0, slice(0, N_TILE), N_TILE)
+        repeated[1] = big.tile([P, SHOT, FEATURES], F32, name="repeated1", tag="big")
+        finish_repeated(1, 0)
         for n in range(1, FEATURE_TILES):
             quantise_and_multiply(PASSES - 1, n)
-        for m in range(EARLY_CLASS_TILES):
-            for n in range(1, FEATURE_TILES):
-                scale_proto(m, n)
-                finish(m, n)
-            store(m, slice(N_TILE, FEATURES), FEATURES - N_TILE)
+        for n in range(1, FEATURE_TILES):
+            scale_proto(0, n)
+            finish(0, n)
+        store(0, slice(N_TILE, FEATURES), FEATURES - N_TILE)
+        for n in range(1, FEATURE_TILES):
+            finish_repeated(1, n)
+        store_repeated(1)
 
         for m in range(EARLY_CLASS_TILES, CLASS_TILES):
+            repeated[m] = big.tile([P, SHOT, FEATURES], F32, name="repeated%d" % m, tag="big")
             for n in range(FEATURE_TILES):
                 open_bank(m, n)
                 for c in range(PASSES):
                     multiply(c, m, n)
-                scale_proto(m, n)
-                finish(m, n)
-            store(m, slice(0, FEATURES), FEATURES)
+                finish_repeated(m, n)
+            store_repeated(m)

@@ -11,6 +11,7 @@ E4M3_X4 = mybir.dt.float8_e4m3fn_x4
 E5M2_X4 = mybir.dt.float8_e5m2_x4
 MULT = mybir.AluOpType.mult
 ADD = mybir.AluOpType.add
+COPY = mybir.ActivationFunctionType.Copy
 
 QUERIES, FEATURES, CLASSES, SHOT = 2048, 1536, 512, 4
 
@@ -21,8 +22,10 @@ PASSES = QUERIES // K_PASS
 N_TILE = 512
 CLASS_TILES = CLASSES // P
 FEATURE_TILES = FEATURES // N_TILE
-EARLY_CLASS_TILES = 2
+ACC_BANKS = 6
 RUN = 4
+VECTOR_COLS = 256
+PLAIN_TILES = 2
 GS_COLS = 32
 
 FLOPS = 2 * QUERIES * CLASSES * FEATURES
@@ -43,21 +46,21 @@ def tile_proto_metric_semi_v_kernel(tc, x1, x2, x3, w, proto, denom, grad_out, o
         stage = ctx.enter_context(tc.tile_pool(name="stage", bufs=4))
         big = ctx.enter_context(tc.tile_pool(name="big", bufs=PASSES))
         diffs = ctx.enter_context(tc.tile_pool(name="diffs", bufs=3))
+        stage_g = ctx.enter_context(tc.tile_pool(name="stage_g", bufs=1))
         psum_acc = ctx.enter_context(
-            tc.psum_pool(name="psum_acc", bufs=EARLY_CLASS_TILES * FEATURE_TILES)
+            tc.psum_pool(name="psum_acc", bufs=ACC_BANKS)
         )
         psum_small = ctx.enter_context(tc.psum_pool(name="psum_small", bufs=1))
+        ctx.enter_context(tc.manual_schedule())
 
-        g_raw = []
-        for c in range(PASSES):
-            g_raw_c = keep.tile([P, PACK, CLASSES], BF16, name="g_raw%d" % c)
-            nc.sync.dma_start(out=g_raw_c[:].rearrange("p j n -> p (j n)"), in_=g_dram[c])
-            g_raw.append(g_raw_c)
         q_raw = []
         for c in range(PASSES):
             q_raw_c = big.tile([P, PACK, FEATURES], BF16, name="q_raw%d" % c, tag="big")
             nc.sync.dma_start(out=q_raw_c[:].rearrange("p j d -> p (j d)"), in_=q_dram[c])
             q_raw.append(q_raw_c)
+        g_raw = keep.tile([P, PASSES, PACK, CLASSES], BF16, name="g_raw")
+        for c in range(PASSES):
+            nc.sync.dma_start(out=g_raw[:, c, :, :].rearrange("p j n -> p (j n)"), in_=g_dram[c])
         proto_sb = []
         for m in range(CLASS_TILES):
             proto_m = keep.tile([P, FEATURES], F32, name="proto%d" % m)
@@ -71,43 +74,63 @@ def tile_proto_metric_semi_v_kernel(tc, x1, x2, x3, w, proto, denom, grad_out, o
         nc.scalar.dma_start(out=denom_rows[0:CLASS_TILES, :], in_=denom_dram)
         ones = keep.tile([P, GS_COLS], BF16, name="ones")
         nc.vector.memset(ones[:], 1.0)
+        denom_ps = psum_small.tile([P, P], F32, name="denom_ps")
+        nc.tensor.transpose(denom_ps[:], denom_rows[:], identity[:])
 
-        g_codes = keep.tile([P, PASSES, CLASSES], U32, name="g_codes", align_bytes=64)
-        g_scales = keep.tile([P, PASSES, CLASSES], U8, name="g_scales", align_bytes=64)
+        g_codes = keep.tile([P, CLASS_TILES, PASSES * P], U32, name="g_codes", align_bytes=64)
+        g_scales = keep.tile([P, CLASS_TILES, PASSES * P], U8, name="g_scales", align_bytes=64)
         q_codes = keep.tile([P, PASSES, FEATURES], U32, name="q_codes", align_bytes=64)
         q_scales = keep.tile([P, PASSES, FEATURES], U8, name="q_scales", align_bytes=64)
 
-        pieces = []
-        for c in range(PASSES):
-            pieces.append((g_raw[c][:, :, :], g_codes[:, c, :], g_scales[:, c, :], E5M2_X4))
-        for c in range(PASSES):
-            for n in range(FEATURE_TILES):
-                cols = slice(n * N_TILE, (n + 1) * N_TILE)
-                pieces.append(
-                    (q_raw[c][:, :, cols], q_codes[:, c, cols], q_scales[:, c, cols], E4M3_X4)
+        q_grouped = {}
+
+        def regroup_q(c, n, engines):
+            if (c, n) not in q_grouped:
+                q_grouped[c, n] = stage.tile(
+                    [P, N_TILE, PACK], BF16, name="grouped", align_bytes=64
                 )
+            grouped = q_grouped[c, n]
+            first = n * N_TILE
+            for engine, copy, lo, hi in (
+                ("vector", nc.vector.tensor_copy, 0, VECTOR_COLS),
+                ("scalar", nc.scalar.copy, VECTOR_COLS, N_TILE),
+            ):
+                if engine in engines:
+                    copy(
+                        out=grouped[:, lo:hi, :].rearrange("p (r i) j -> p r j i", i=RUN),
+                        in_=q_raw[c][:, :, first + lo : first + hi].rearrange(
+                            "p j (r i) -> p r j i", i=RUN
+                        ),
+                    )
 
-        def regroup(index):
-            source = pieces[index][0]
-            grouped = stage.tile([P, N_TILE, PACK], BF16, name="grouped", align_bytes=64)
-            on_vector = index % 2 == 1 and index != len(pieces) - 1
-            copy = nc.vector.tensor_copy if on_vector else nc.scalar.copy
-            copy(
-                out=grouped[:].rearrange("p (r i) j -> p r j i", i=RUN),
-                in_=source.rearrange("p j (r i) -> p r j i", i=RUN),
-            )
-            return grouped
-
-        regrouped = [regroup(0)]
-
-        def quantise(index):
-            if index + 1 < len(pieces):
-                regrouped.append(regroup(index + 1))
-            words, scale_bytes, packed = pieces[index][1:]
+        def quantise_q(c, n):
+            cols = slice(n * N_TILE, (n + 1) * N_TILE)
             nc.vector.quantize_mx(
-                out=words.bitcast(packed),
-                scales=scale_bytes,
-                in_=regrouped[index][:].rearrange("p col j -> p (col j)"),
+                out=q_codes[:, c, cols].bitcast(E4M3_X4),
+                scales=q_scales[:, c, cols],
+                in_=q_grouped[c, n][:].rearrange("p col j -> p (col j)"),
+            )
+
+        g_grouped = []
+        for m in range(CLASS_TILES):
+            g_grouped.append(
+                stage_g.tile([P, PASSES * P, PACK], BF16, name="g_grouped%d" % m, align_bytes=64)
+            )
+
+        def regroup_g(copy, m, c_lo, c_hi):
+            copy(
+                out=g_grouped[m][:, c_lo * P : c_hi * P, :].rearrange(
+                    "p (c n) j -> p c n j", c=c_hi - c_lo
+                ),
+                in_=g_raw[:, c_lo:c_hi, :, m * P : (m + 1) * P].rearrange("p c j n -> p c n j"),
+            )
+
+        def quantise_g(m, c_lo, c_hi):
+            cols = slice(c_lo * P, c_hi * P)
+            nc.vector.quantize_mx(
+                out=g_codes[:, m, cols].bitcast(E5M2_X4),
+                scales=g_scales[:, m, cols],
+                in_=g_grouped[m][:, cols, :].rearrange("p col j -> p (col j)"),
             )
 
         acc = {}
@@ -118,32 +141,51 @@ def tile_proto_metric_semi_v_kernel(tc, x1, x2, x3, w, proto, denom, grad_out, o
         def multiply(c, m, n):
             nc.tensor.matmul_mx(
                 out=acc[m, n][:],
-                lhsT=g_codes[:, c, m * P : (m + 1) * P].bitcast(E5M2_X4),
-                lhsT_scale=g_scales[:, c, m * P : (m + 1) * P],
+                lhsT=g_codes[:, m, c * P : (c + 1) * P].bitcast(E5M2_X4),
+                lhsT_scale=g_scales[:, m, c * P : (c + 1) * P],
                 rhs=q_codes[:, c, n * N_TILE : (n + 1) * N_TILE].bitcast(E4M3_X4),
                 rhs_scale=q_scales[:, c, n * N_TILE : (n + 1) * N_TILE],
                 start=(c == 0),
                 stop=(c == PASSES - 1),
             )
 
-        result = [keep.tile([P, FEATURES], F32, name="result0")]
+        gs_ps = psum_small.tile([P, CLASS_TILES, GS_COLS], F32, name="gs_ps")
+
+        def sum_grad_out(m):
+            for c in range(PASSES):
+                for j in range(PACK):
+                    nc.tensor.matmul(
+                        out=gs_ps[:, m, :],
+                        lhsT=g_raw[:, c, j, m * P : (m + 1) * P],
+                        rhs=ones[:],
+                        start=(c == 0 and j == 0),
+                        stop=(c == PASSES - 1 and j == PACK - 1),
+                    )
+
+        result = []
+        for m in range(PLAIN_TILES):
+            result.append(keep.tile([P, FEATURES], F32, name="result%d" % m))
+        proto_factor = keep.tile([P, PLAIN_TILES], F32, name="proto_factor")
         repeated = {}
+
+        def make_proto_factor(m):
+            nc.vector.scalar_tensor_tensor(
+                out=proto_factor[:, m : m + 1],
+                in0=gs_ps[:, m, 0:1],
+                scalar=-1.0,
+                in1=two_over_denom[:, m : m + 1],
+                op0=MULT,
+                op1=MULT,
+            )
 
         def scale_proto(m, n):
             cols = slice(n * N_TILE, (n + 1) * N_TILE)
-            if n == 0:
-                nc.vector.tensor_scalar_mul(
-                    out=proto_sb[m][:, cols],
-                    in0=proto_sb[m][:, cols],
-                    scalar1=proto_factor[:, m : m + 1],
-                )
-            else:
-                nc.scalar.activation(
-                    out=proto_sb[m][:, cols],
-                    in_=proto_sb[m][:, cols],
-                    func=mybir.ActivationFunctionType.Copy,
-                    scale=proto_factor[:, m : m + 1],
-                )
+            nc.scalar.activation(
+                out=proto_sb[m][:, cols],
+                in_=proto_sb[m][:, cols],
+                func=COPY,
+                scale=proto_factor[:, m : m + 1],
+            )
 
         def finish(m, n):
             cols = slice(n * N_TILE, (n + 1) * N_TILE)
@@ -154,6 +196,12 @@ def tile_proto_metric_semi_v_kernel(tc, x1, x2, x3, w, proto, denom, grad_out, o
                 in1=proto_sb[m][:, cols],
                 op0=MULT,
                 op1=ADD,
+            )
+
+        def store(m, lo, hi):
+            nc.sync.dma_start(
+                out=out_dram[m][:, :, lo:hi],
+                in_=result[m][:, lo:hi].unsqueeze(1).to_broadcast([P, SHOT, hi - lo]),
             )
 
         def finish_repeated(m, n):
@@ -172,7 +220,7 @@ def tile_proto_metric_semi_v_kernel(tc, x1, x2, x3, w, proto, denom, grad_out, o
             nc.scalar.activation(
                 out=repeated[m][:, 0:half, cols],
                 in_=twice,
-                func=mybir.ActivationFunctionType.Copy,
+                func=COPY,
                 scale=two_over_denom[:, m : m + 1],
             )
             nc.vector.tensor_scalar_mul(
@@ -187,66 +235,89 @@ def tile_proto_metric_semi_v_kernel(tc, x1, x2, x3, w, proto, denom, grad_out, o
                 in_=repeated[m][:].rearrange("p s d -> p (s d)"),
             )
 
-        def store(m, cols, width):
-            nc.sync.dma_start(
-                out=out_dram[m][:, :, cols],
-                in_=result[m][:, cols].unsqueeze(1).to_broadcast([P, SHOT, width]),
-            )
-
-        for c in range(PASSES):
-            quantise(c)
-        gs_ps = psum_small.tile([P, CLASS_TILES, GS_COLS], F32, name="gs_ps")
-        for m in range(CLASS_TILES):
-            for c in range(PASSES):
-                for j in range(PACK):
-                    nc.tensor.matmul(
-                        out=gs_ps[:, m, :],
-                        lhsT=g_raw[c][:, j, m * P : (m + 1) * P],
-                        rhs=ones[:],
-                        start=(c == 0 and j == 0),
-                        stop=(c == PASSES - 1 and j == PACK - 1),
-                    )
-        denom_ps = psum_small.tile([P, P], F32, name="denom_ps")
-        nc.tensor.transpose(denom_ps[:], denom_rows[:], identity[:])
-
-        def quantise_and_multiply(c, n):
-            quantise(PASSES + c * FEATURE_TILES + n)
-            for m in range(EARLY_CLASS_TILES):
-                multiply(c, m, n)
-
-        for m in range(EARLY_CLASS_TILES):
-            for n in range(FEATURE_TILES):
-                open_bank(m, n)
-        for c in range(PASSES - 1):
-            for n in range(FEATURE_TILES):
-                quantise_and_multiply(c, n)
-
-        one_over_denom = keep.tile([P, CLASS_TILES], F32, name="one_over_denom")
-        nc.vector.reciprocal(out=one_over_denom[:], in_=denom_ps[:, 0:CLASS_TILES])
-        two_over_denom = keep.tile([P, CLASS_TILES], F32, name="two_over_denom")
-        nc.vector.tensor_scalar_mul(out=two_over_denom[:], in0=one_over_denom[:], scalar1=2.0)
-        minus_gs = keep.tile([P, CLASS_TILES], F32, name="minus_gs")
-        nc.vector.tensor_scalar_mul(out=minus_gs[:], in0=gs_ps[:, :, 0], scalar1=-1.0)
-        proto_factor = keep.tile([P, CLASS_TILES], F32, name="proto_factor")
-        nc.vector.tensor_mul(out=proto_factor[:], in0=minus_gs[:], in1=two_over_denom[:])
-
-        quantise_and_multiply(PASSES - 1, 0)
-        scale_proto(0, 0)
-        finish(0, 0)
-        store(0, slice(0, N_TILE), N_TILE)
-        repeated[1] = big.tile([P, SHOT, FEATURES], F32, name="repeated1", tag="big")
-        finish_repeated(1, 0)
-        for n in range(1, FEATURE_TILES):
-            quantise_and_multiply(PASSES - 1, n)
-        for n in range(1, FEATURE_TILES):
+        both = ("vector", "scalar")
+        last = PASSES - 1
+        early = FEATURE_TILES - 1
+        for n in range(FEATURE_TILES):
+            open_bank(0, n)
+        regroup_q(0, 0, both)
+        for c in range(last):
+            regroup_q(c, 1, both)
+            quantise_q(c, 0)
+            regroup_q(c, 2, both)
+            quantise_q(c, 1)
+            regroup_q(c + 1, 0, both)
+            if c == last - 1:
+                one_over_denom = keep.tile([P, CLASS_TILES], F32, name="one_over_denom")
+                nc.vector.reciprocal(out=one_over_denom[:], in_=denom_ps[:, 0:CLASS_TILES])
+                two_over_denom = keep.tile([P, CLASS_TILES], F32, name="two_over_denom")
+                nc.vector.tensor_scalar_mul(
+                    out=two_over_denom[:], in0=one_over_denom[:], scalar1=2.0
+                )
+            quantise_q(c, 2)
+        regroup_g(nc.vector.tensor_copy, 0, 0, 1)
+        regroup_q(last, 1, both)
+        quantise_g(0, 0, 1)
+        for n in range(early):
+            multiply(0, 0, n)
+        regroup_g(nc.vector.tensor_copy, 0, 1, 2)
+        quantise_q(last, 0)
+        quantise_g(0, 1, 2)
+        sum_grad_out(0)
+        for n in range(early):
+            multiply(1, 0, n)
+        regroup_q(last, 2, ("scalar",))
+        regroup_g(nc.vector.tensor_copy, 0, 2, 3)
+        regroup_g(nc.vector.tensor_copy, 0, 3, PASSES)
+        quantise_g(0, 2, 3)
+        for n in range(early):
+            multiply(2, 0, n)
+        make_proto_factor(0)
+        quantise_g(0, 3, PASSES)
+        multiply(last, 0, 0)
+        quantise_q(last, 1)
+        multiply(last, 0, 1)
+        for n in range(early):
             scale_proto(0, n)
             finish(0, n)
-        store(0, slice(N_TILE, FEATURES), FEATURES - N_TILE)
-        for n in range(1, FEATURE_TILES):
-            finish_repeated(1, n)
-        store_repeated(1)
+        store(0, 0, early * N_TILE)
 
-        for m in range(EARLY_CLASS_TILES, CLASS_TILES):
+        for c in range(last):
+            multiply(c, 0, early)
+        for m in range(1, CLASS_TILES):
+            sum_grad_out(m)
+        regroup_g(nc.scalar.copy, 1, 2, PASSES)
+        scale_proto(0, early)
+        regroup_g(nc.vector.tensor_copy, 1, 0, 2)
+        make_proto_factor(1)
+        regroup_q(last, 2, ("vector",))
+        quantise_g(1, 0, PASSES)
+        quantise_q(last, 2)
+        minus_gs = keep.tile([P, CLASS_TILES], F32, name="minus_gs")
+        nc.vector.tensor_scalar_mul(out=minus_gs[:], in0=gs_ps[:, :, 0], scalar1=-1.0)
+        regroup_g(nc.scalar.copy, 2, 2, PASSES)
+        for n in range(FEATURE_TILES):
+            open_bank(1, n)
+            scale_proto(1, n)
+        regroup_g(nc.scalar.copy, 3, 2, PASSES)
+        for c in range(PASSES):
+            multiply(c, 1, 0)
+        multiply(last, 0, early)
+        finish(1, 0)
+        finish(0, early)
+        store(0, early * N_TILE, FEATURES)
+        regroup_g(nc.vector.tensor_copy, 2, 0, 2)
+        for n in range(1, FEATURE_TILES):
+            for c in range(PASSES):
+                multiply(c, 1, n)
+            finish(1, n)
+            if n == 1:
+                quantise_g(2, 0, PASSES)
+        store(1, 0, FEATURES)
+        regroup_g(nc.vector.tensor_copy, 3, 0, 2)
+        quantise_g(3, 0, PASSES)
+
+        for m in range(PLAIN_TILES, CLASS_TILES):
             repeated[m] = big.tile([P, SHOT, FEATURES], F32, name="repeated%d" % m, tag="big")
             for n in range(FEATURE_TILES):
                 open_bank(m, n)

@@ -149,13 +149,16 @@ def tile_proto_metric_semi_v_kernel(tc, x1, x2, x3, w, proto, denom, grad_out, o
                 stop=(c == PASSES - 1),
             )
 
-        gs_ps = psum_small.tile([P, CLASS_TILES, GS_COLS], F32, name="gs_ps")
+        gs_banks = [psum_small.tile([P, 2, GS_COLS], F32, name="gs_even")]
 
-        def sum_grad_out(m):
-            for c in range(PASSES):
+        def gs_of(m):
+            return gs_banks[m % 2][:, m // 2, :]
+
+        def sum_grad_out(m, c_lo, c_hi):
+            for c in range(c_lo, c_hi):
                 for j in range(PACK):
                     nc.tensor.matmul(
-                        out=gs_ps[:, m, :],
+                        out=gs_of(m),
                         lhsT=g_raw[:, c, j, m * P : (m + 1) * P],
                         rhs=ones[:],
                         start=(c == 0 and j == 0),
@@ -171,7 +174,7 @@ def tile_proto_metric_semi_v_kernel(tc, x1, x2, x3, w, proto, denom, grad_out, o
         def make_proto_factor(m):
             nc.vector.scalar_tensor_tensor(
                 out=proto_factor[:, m : m + 1],
-                in0=gs_ps[:, m, 0:1],
+                in0=gs_of(m)[:, 0:1],
                 scalar=-1.0,
                 in1=two_over_denom[:, m : m + 1],
                 op0=MULT,
@@ -202,6 +205,13 @@ def tile_proto_metric_semi_v_kernel(tc, x1, x2, x3, w, proto, denom, grad_out, o
             nc.sync.dma_start(
                 out=out_dram[m][:, :, lo:hi],
                 in_=result[m][:, lo:hi].unsqueeze(1).to_broadcast([P, SHOT, hi - lo]),
+            )
+
+        minus_gs = keep.tile([P, CLASS_TILES], F32, name="minus_gs")
+
+        def make_minus_gs(m):
+            nc.vector.tensor_scalar_mul(
+                out=minus_gs[:, m : m + 1], in0=gs_of(m)[:, 0:1], scalar1=-1.0
             )
 
         def finish_repeated(m, n):
@@ -258,18 +268,20 @@ def tile_proto_metric_semi_v_kernel(tc, x1, x2, x3, w, proto, denom, grad_out, o
         regroup_g(nc.vector.tensor_copy, 0, 0, 1)
         regroup_q(last, 1, both)
         quantise_g(0, 0, 1)
+        sum_grad_out(0, 0, 1)
         for n in range(early):
             multiply(0, 0, n)
         regroup_g(nc.vector.tensor_copy, 0, 1, 2)
         quantise_q(last, 0)
         quantise_g(0, 1, 2)
-        sum_grad_out(0)
+        sum_grad_out(0, 1, 2)
         for n in range(early):
             multiply(1, 0, n)
         regroup_q(last, 2, ("scalar",))
         regroup_g(nc.vector.tensor_copy, 0, 2, 3)
         regroup_g(nc.vector.tensor_copy, 0, 3, PASSES)
         quantise_g(0, 2, 3)
+        sum_grad_out(0, 2, PASSES)
         for n in range(early):
             multiply(2, 0, n)
         make_proto_factor(0)
@@ -282,23 +294,22 @@ def tile_proto_metric_semi_v_kernel(tc, x1, x2, x3, w, proto, denom, grad_out, o
             finish(0, n)
         store(0, 0, early * N_TILE)
 
+        gs_banks.append(psum_small.tile([P, 2, GS_COLS], F32, name="gs_odd", tag="denom_ps"))
+        sum_grad_out(1, 0, PASSES)
         for c in range(last):
             multiply(c, 0, early)
-        for m in range(1, CLASS_TILES):
-            sum_grad_out(m)
+        sum_grad_out(2, 0, PASSES)
         regroup_g(nc.scalar.copy, 1, 2, PASSES)
         scale_proto(0, early)
         regroup_g(nc.vector.tensor_copy, 1, 0, 2)
-        make_proto_factor(1)
         regroup_q(last, 2, ("vector",))
+        make_proto_factor(1)
         quantise_g(1, 0, PASSES)
         quantise_q(last, 2)
-        minus_gs = keep.tile([P, CLASS_TILES], F32, name="minus_gs")
-        nc.vector.tensor_scalar_mul(out=minus_gs[:], in0=gs_ps[:, :, 0], scalar1=-1.0)
-        regroup_g(nc.scalar.copy, 2, 2, PASSES)
         for n in range(FEATURE_TILES):
             open_bank(1, n)
             scale_proto(1, n)
+        regroup_g(nc.scalar.copy, 2, 2, PASSES)
         regroup_g(nc.scalar.copy, 3, 2, PASSES)
         for c in range(PASSES):
             multiply(c, 1, 0)
@@ -306,15 +317,17 @@ def tile_proto_metric_semi_v_kernel(tc, x1, x2, x3, w, proto, denom, grad_out, o
         finish(1, 0)
         finish(0, early)
         store(0, early * N_TILE, FEATURES)
+        for c in range(PASSES):
+            multiply(c, 1, 1)
+        finish(1, 1)
         regroup_g(nc.vector.tensor_copy, 2, 0, 2)
-        for n in range(1, FEATURE_TILES):
-            for c in range(PASSES):
-                multiply(c, 1, n)
-            finish(1, n)
-            if n == 1:
-                quantise_g(2, 0, PASSES)
+        for c in range(PASSES):
+            multiply(c, 1, 2)
+        finish(1, 2)
         store(1, 0, FEATURES)
+        quantise_g(2, 0, PASSES)
         regroup_g(nc.vector.tensor_copy, 3, 0, 2)
+        make_minus_gs(2)
         quantise_g(3, 0, PASSES)
 
         for m in range(PLAIN_TILES, CLASS_TILES):
@@ -325,3 +338,6 @@ def tile_proto_metric_semi_v_kernel(tc, x1, x2, x3, w, proto, denom, grad_out, o
                     multiply(c, m, n)
                 finish_repeated(m, n)
             store_repeated(m)
+            if m == PLAIN_TILES:
+                sum_grad_out(3, 0, PASSES)
+                make_minus_gs(3)

@@ -36,8 +36,8 @@ def tile_proto_metric_semi_v_kernel(tc, x1, x2, x3, w, proto, denom, grad_out, o
     nc = tc.nc
 
     q_dram = x1.rearrange("(c p j) d a b -> c p (j d a b)", p=P, j=PACK)
-    g_dram = grad_out.rearrange("(c p j) n -> c p (j n)", p=P, j=PACK)
-    proto_dram = proto.rearrange("(m p) d -> m p d", p=P)
+    g_dram = grad_out.rearrange("(c p j) n -> p c (j n)", p=P, j=PACK)
+    proto_dram = proto.rearrange("(m p) d -> p m d", p=P)
     denom_dram = denom.rearrange("(m p) -> m p", p=P)
     out_dram = out.rearrange("(m p) s d -> m p s d", p=P)
 
@@ -59,13 +59,17 @@ def tile_proto_metric_semi_v_kernel(tc, x1, x2, x3, w, proto, denom, grad_out, o
             nc.sync.dma_start(out=q_raw_c[:].rearrange("p j d -> p (j d)"), in_=q_dram[c])
             q_raw.append(q_raw_c)
         g_raw = keep.tile([P, PASSES, PACK, CLASSES], BF16, name="g_raw")
-        for c in range(PASSES):
-            nc.sync.dma_start(out=g_raw[:, c, :, :].rearrange("p j n -> p (j n)"), in_=g_dram[c])
+        for c in range(0, PASSES, 2):
+            nc.sync.dma_start(
+                out=g_raw[:, c : c + 2, :, :].rearrange("p c j n -> p c (j n)"),
+                in_=g_dram[:, c : c + 2, :],
+            )
+        proto_all = keep.tile([P, CLASS_TILES, FEATURES], F32, name="proto_all")
+        for m_lo, m_hi in ((0, 1), (1, 2), (2, CLASS_TILES)):
+            nc.sync.dma_start(out=proto_all[:, m_lo:m_hi, :], in_=proto_dram[:, m_lo:m_hi, :])
         proto_sb = []
         for m in range(CLASS_TILES):
-            proto_m = keep.tile([P, FEATURES], F32, name="proto%d" % m)
-            nc.sync.dma_start(out=proto_m[:], in_=proto_dram[m])
-            proto_sb.append(proto_m)
+            proto_sb.append(proto_all[:, m, :])
 
         identity = keep.tile([P, P], F32, name="identity")
         make_identity(nc, identity[:])
@@ -201,8 +205,8 @@ def tile_proto_metric_semi_v_kernel(tc, x1, x2, x3, w, proto, denom, grad_out, o
                 op1=ADD,
             )
 
-        def store(m, lo, hi):
-            nc.sync.dma_start(
+        def store(queue, m, lo, hi):
+            queue.dma_start(
                 out=out_dram[m][:, :, lo:hi],
                 in_=result[m][:, lo:hi].unsqueeze(1).to_broadcast([P, SHOT, hi - lo]),
             )
@@ -239,8 +243,8 @@ def tile_proto_metric_semi_v_kernel(tc, x1, x2, x3, w, proto, denom, grad_out, o
                 scalar1=two_over_denom[:, m : m + 1],
             )
 
-        def store_repeated(m):
-            nc.sync.dma_start(
+        def store_repeated(queue, m):
+            queue.dma_start(
                 out=out_dram[m].rearrange("p s d -> p (s d)"),
                 in_=repeated[m][:].rearrange("p s d -> p (s d)"),
             )
@@ -265,34 +269,27 @@ def tile_proto_metric_semi_v_kernel(tc, x1, x2, x3, w, proto, denom, grad_out, o
                     out=two_over_denom[:], in0=one_over_denom[:], scalar1=2.0
                 )
             quantise_q(c, 2)
-        regroup_g(nc.vector.tensor_copy, 0, 0, 1)
+        regroup_g(nc.vector.tensor_copy, 0, 0, 2)
         regroup_q(last, 1, both)
-        quantise_g(0, 0, 1)
-        sum_grad_out(0, 0, 1)
-        for n in range(early):
-            multiply(0, 0, n)
-        regroup_g(nc.vector.tensor_copy, 0, 1, 2)
+        quantise_g(0, 0, 2)
+        sum_grad_out(0, 0, 2)
+        for c in range(2):
+            for n in range(early):
+                multiply(c, 0, n)
         quantise_q(last, 0)
-        quantise_g(0, 1, 2)
-        sum_grad_out(0, 1, 2)
-        for n in range(early):
-            multiply(1, 0, n)
         regroup_q(last, 2, ("scalar",))
-        regroup_g(nc.vector.tensor_copy, 0, 2, 3)
-        regroup_g(nc.vector.tensor_copy, 0, 3, PASSES)
-        quantise_g(0, 2, 3)
+        regroup_g(nc.vector.tensor_copy, 0, 2, PASSES)
+        quantise_q(last, 1)
+        quantise_g(0, 2, PASSES)
         sum_grad_out(0, 2, PASSES)
+        make_proto_factor(0)
         for n in range(early):
             multiply(2, 0, n)
-        make_proto_factor(0)
-        quantise_g(0, 3, PASSES)
-        multiply(last, 0, 0)
-        quantise_q(last, 1)
-        multiply(last, 0, 1)
+            multiply(last, 0, n)
         for n in range(early):
             scale_proto(0, n)
             finish(0, n)
-        store(0, 0, early * N_TILE)
+        store(nc.sync, 0, 0, early * N_TILE)
 
         gs_banks.append(psum_small.tile([P, 2, GS_COLS], F32, name="gs_odd", tag="denom_ps"))
         sum_grad_out(1, 0, PASSES)
@@ -316,7 +313,7 @@ def tile_proto_metric_semi_v_kernel(tc, x1, x2, x3, w, proto, denom, grad_out, o
         multiply(last, 0, early)
         finish(1, 0)
         finish(0, early)
-        store(0, early * N_TILE, FEATURES)
+        store(nc.sync, 0, early * N_TILE, FEATURES)
         for c in range(PASSES):
             multiply(c, 1, 1)
         finish(1, 1)
@@ -324,7 +321,7 @@ def tile_proto_metric_semi_v_kernel(tc, x1, x2, x3, w, proto, denom, grad_out, o
         for c in range(PASSES):
             multiply(c, 1, 2)
         finish(1, 2)
-        store(1, 0, FEATURES)
+        store(nc.scalar, 1, 0, FEATURES)
         quantise_g(2, 0, PASSES)
         regroup_g(nc.vector.tensor_copy, 3, 0, 2)
         make_minus_gs(2)
@@ -337,7 +334,7 @@ def tile_proto_metric_semi_v_kernel(tc, x1, x2, x3, w, proto, denom, grad_out, o
                 for c in range(PASSES):
                     multiply(c, m, n)
                 finish_repeated(m, n)
-            store_repeated(m)
+            store_repeated(nc.sync if m == PLAIN_TILES else nc.scalar, m)
             if m == PLAIN_TILES:
                 sum_grad_out(3, 0, PASSES)
                 make_minus_gs(3)

@@ -1,7 +1,6 @@
 from contextlib import ExitStack
 
 import concourse.mybir as mybir
-from concourse.masks import make_identity
 
 F32 = mybir.dt.float32
 BF16 = mybir.dt.bfloat16
@@ -71,15 +70,20 @@ def tile_proto_metric_semi_v_kernel(tc, x1, x2, x3, w, proto, denom, grad_out, o
         for m in range(CLASS_TILES):
             proto_sb.append(proto_all[:, m, :])
 
-        identity = keep.tile([P, P], F32, name="identity")
-        make_identity(nc, identity[:])
+        QUADRANT = P // CLASS_TILES
         denom_rows = keep.tile([P, P], F32, name="denom_rows")
         nc.vector.memset(denom_rows[:], 0.0)
-        nc.scalar.dma_start(out=denom_rows[0:CLASS_TILES, :], in_=denom_dram)
+        nc.scalar.dma_start(out=denom_rows[0:P:QUADRANT, :], in_=denom_dram)
+        selector = keep.tile([P, CLASS_TILES], F32, name="selector")
+        nc.vector.memset(selector[:], 0.0)
+        for m in range(CLASS_TILES):
+            nc.vector.memset(selector[m * QUADRANT : m * QUADRANT + 1, m : m + 1], 1.0)
         ones = keep.tile([P, GS_COLS], BF16, name="ones")
         nc.vector.memset(ones[:], 1.0)
         denom_ps = psum_small.tile([P, P], F32, name="denom_ps")
-        nc.tensor.transpose(denom_ps[:], denom_rows[:], identity[:])
+        nc.tensor.matmul(
+            out=denom_ps[:, 0:CLASS_TILES], lhsT=denom_rows[:], rhs=selector[:], start=True, stop=True
+        )
 
         g_codes = keep.tile([P, CLASS_TILES, PASSES * P], U32, name="g_codes", align_bytes=64)
         g_scales = keep.tile([P, CLASS_TILES, PASSES * P], U8, name="g_scales", align_bytes=64)

from contextlib import ExitStack

import concourse.mybir as mybir

F32 = mybir.dt.float32
BF16 = mybir.dt.bfloat16
U32 = mybir.dt.uint32
U8 = mybir.dt.uint8
E4M3_X4 = mybir.dt.float8_e4m3fn_x4
E5M2_X4 = mybir.dt.float8_e5m2_x4
MULT = mybir.AluOpType.mult
ADD = mybir.AluOpType.add
COPY = mybir.ActivationFunctionType.Copy

QUERIES, FEATURES, CLASSES, SHOT = 2048, 1536, 512, 4

P = 128
PACK = 4
K_PASS = P * PACK
PASSES = QUERIES // K_PASS
N_TILE = 512
CLASS_TILES = CLASSES // P
FEATURE_TILES = FEATURES // N_TILE
ACC_BANKS = 6
RUN = 4
VECTOR_COLS = 256
PLAIN_TILES = 2
GS_COLS = 32

FLOPS = 2 * QUERIES * CLASSES * FEATURES
BYTES = 2 * QUERIES * (FEATURES + CLASSES) + 4 * CLASSES * (FEATURES + 1 + SHOT * FEATURES)


def tile_proto_metric_semi_v_kernel(tc, x1, x2, x3, w, proto, denom, grad_out, out):
    nc = tc.nc

    q_dram = x1.rearrange("(c p j) d a b -> c p (j d a b)", p=P, j=PACK)
    g_dram = grad_out.rearrange("(c p j) n -> p c (j n)", p=P, j=PACK)
    proto_dram = proto.rearrange("(m p) d -> p m d", p=P)
    denom_dram = denom.rearrange("(m p) -> m p", p=P)
    out_dram = out.rearrange("(m p) s d -> m p s d", p=P)

    with ExitStack() as ctx:
        keep = ctx.enter_context(tc.tile_pool(name="keep", bufs=1))
        stage = ctx.enter_context(tc.tile_pool(name="stage", bufs=4))
        big = ctx.enter_context(tc.tile_pool(name="big", bufs=PASSES))
        diffs = ctx.enter_context(tc.tile_pool(name="diffs", bufs=3))
        stage_g = ctx.enter_context(tc.tile_pool(name="stage_g", bufs=1))
        psum_acc = ctx.enter_context(
            tc.psum_pool(name="psum_acc", bufs=ACC_BANKS)
        )
        psum_small = ctx.enter_context(tc.psum_pool(name="psum_small", bufs=1))
        ctx.enter_context(tc.manual_schedule())

        q_raw = []
        for c in range(PASSES):
            q_raw_c = big.tile([P, PACK, FEATURES], BF16, name="q_raw%d" % c, tag="big")
            nc.sync.dma_start(out=q_raw_c[:].rearrange("p j d -> p (j d)"), in_=q_dram[c])
            q_raw.append(q_raw_c)
        g_raw = keep.tile([P, PASSES, PACK, CLASSES], BF16, name="g_raw")
        for c in range(0, PASSES, 2):
            nc.sync.dma_start(
                out=g_raw[:, c : c + 2, :, :].rearrange("p c j n -> p c (j n)"),
                in_=g_dram[:, c : c + 2, :],
            )
        proto_all = keep.tile([P, CLASS_TILES, FEATURES], F32, name="proto_all")
        for m_lo, m_hi in ((0, 1), (1, 2), (2, CLASS_TILES)):
            nc.sync.dma_start(out=proto_all[:, m_lo:m_hi, :], in_=proto_dram[:, m_lo:m_hi, :])
        proto_sb = []
        for m in range(CLASS_TILES):
            proto_sb.append(proto_all[:, m, :])

        QUADRANT = P // CLASS_TILES
        denom_rows = keep.tile([P, P], F32, name="denom_rows")
        nc.vector.memset(denom_rows[:], 0.0)
        nc.scalar.dma_start(out=denom_rows[0:P:QUADRANT, :], in_=denom_dram)
        selector = keep.tile([P, CLASS_TILES], F32, name="selector")
        nc.vector.memset(selector[:], 0.0)
        for m in range(CLASS_TILES):
            nc.vector.memset(selector[m * QUADRANT : m * QUADRANT + 1, m : m + 1], 1.0)
        ones = keep.tile([P, GS_COLS], BF16, name="ones")
        nc.vector.memset(ones[:], 1.0)
        denom_ps = psum_small.tile([P, P], F32, name="denom_ps")
        nc.tensor.matmul(
            out=denom_ps[:, 0:CLASS_TILES], lhsT=denom_rows[:], rhs=selector[:], start=True, stop=True
        )

        g_codes = keep.tile([P, CLASS_TILES, PASSES * P], U32, name="g_codes", align_bytes=64)
        g_scales = keep.tile([P, CLASS_TILES, PASSES * P], U8, name="g_scales", align_bytes=64)
        q_codes = keep.tile([P, PASSES, FEATURES], U32, name="q_codes", align_bytes=64)
        q_scales = keep.tile([P, PASSES, FEATURES], U8, name="q_scales", align_bytes=64)

        q_grouped = {}

        def regroup_q(c, n, engines):
            if (c, n) not in q_grouped:
                q_grouped[c, n] = stage.tile(
                    [P, N_TILE, PACK], BF16, name="grouped", align_bytes=64
                )
            grouped = q_grouped[c, n]
            first = n * N_TILE
            for engine, copy, lo, hi in (
                ("vector", nc.vector.tensor_copy, 0, VECTOR_COLS),
                ("scalar", nc.scalar.copy, VECTOR_COLS, N_TILE),
            ):
                if engine in engines:
                    copy(
                        out=grouped[:, lo:hi, :].rearrange("p (r i) j -> p r j i", i=RUN),
                        in_=q_raw[c][:, :, first + lo : first + hi].rearrange(
                            "p j (r i) -> p r j i", i=RUN
                        ),
                    )

        def quantise_q(c, n):
            cols = slice(n * N_TILE, (n + 1) * N_TILE)
            nc.vector.quantize_mx(
                out=q_codes[:, c, cols].bitcast(E4M3_X4),
                scales=q_scales[:, c, cols],
                in_=q_grouped[c, n][:].rearrange("p col j -> p (col j)"),
            )

        g_grouped = []
        for m in range(CLASS_TILES):
            g_grouped.append(
                stage_g.tile([P, PASSES * P, PACK], BF16, name="g_grouped%d" % m, align_bytes=64)
            )

        def regroup_g(copy, m, c_lo, c_hi):
            copy(
                out=g_grouped[m][:, c_lo * P : c_hi * P, :].rearrange(
                    "p (c n) j -> p c n j", c=c_hi - c_lo
                ),
                in_=g_raw[:, c_lo:c_hi, :, m * P : (m + 1) * P].rearrange("p c j n -> p c n j"),
            )

        def quantise_g(m, c_lo, c_hi):
            cols = slice(c_lo * P, c_hi * P)
            nc.vector.quantize_mx(
                out=g_codes[:, m, cols].bitcast(E5M2_X4),
                scales=g_scales[:, m, cols],
                in_=g_grouped[m][:, cols, :].rearrange("p col j -> p (col j)"),
            )

        acc = {}

        def open_bank(m, n):
            acc[m, n] = psum_acc.tile([P, N_TILE], F32, name="acc_%d_%d" % (m, n), tag="acc")

        def multiply(c, m, n):
            nc.tensor.matmul_mx(
                out=acc[m, n][:],
                lhsT=g_codes[:, m, c * P : (c + 1) * P].bitcast(E5M2_X4),
                lhsT_scale=g_scales[:, m, c * P : (c + 1) * P],
                rhs=q_codes[:, c, n * N_TILE : (n + 1) * N_TILE].bitcast(E4M3_X4),
                rhs_scale=q_scales[:, c, n * N_TILE : (n + 1) * N_TILE],
                start=(c == 0),
                stop=(c == PASSES - 1),
            )

        gs_banks = [psum_small.tile([P, 2, GS_COLS], F32, name="gs_even")]

        def gs_of(m):
            return gs_banks[m % 2][:, m // 2, :]

        def sum_grad_out(m, c_lo, c_hi):
            for c in range(c_lo, c_hi):
                for j in range(PACK):
                    nc.tensor.matmul(
                        out=gs_of(m),
                        lhsT=g_raw[:, c, j, m * P : (m + 1) * P],
                        rhs=ones[:],
                        start=(c == 0 and j == 0),
                        stop=(c == PASSES - 1 and j == PACK - 1),
                    )

        result = []
        for m in range(PLAIN_TILES):
            result.append(keep.tile([P, FEATURES], F32, name="result%d" % m))
        proto_factor = keep.tile([P, PLAIN_TILES], F32, name="proto_factor")
        repeated = {}

        def make_proto_factor(m):
            nc.vector.scalar_tensor_tensor(
                out=proto_factor[:, m : m + 1],
                in0=gs_of(m)[:, 0:1],
                scalar=-1.0,
                in1=two_over_denom[:, m : m + 1],
                op0=MULT,
                op1=MULT,
            )

        def scale_proto(m, n):
            cols = slice(n * N_TILE, (n + 1) * N_TILE)
            nc.scalar.activation(
                out=proto_sb[m][:, cols],
                in_=proto_sb[m][:, cols],
                func=COPY,
                scale=proto_factor[:, m : m + 1],
            )

        def finish(m, n):
            cols = slice(n * N_TILE, (n + 1) * N_TILE)
            nc.vector.scalar_tensor_tensor(
                out=result[m][:, cols],
                in0=acc[m, n][:],
                scalar=two_over_denom[:, m : m + 1],
                in1=proto_sb[m][:, cols],
                op0=MULT,
                op1=ADD,
            )

        def store(queue, m, lo, hi):
            queue.dma_start(
                out=out_dram[m][:, :, lo:hi],
                in_=result[m][:, lo:hi].unsqueeze(1).to_broadcast([P, SHOT, hi - lo]),
            )

        minus_gs = keep.tile([P, CLASS_TILES], F32, name="minus_gs")

        def make_minus_gs(m):
            nc.vector.tensor_scalar_mul(
                out=minus_gs[:, m : m + 1], in0=gs_of(m)[:, 0:1], scalar1=-1.0
            )

        def finish_repeated(m, n):
            cols = slice(n * N_TILE, (n + 1) * N_TILE)
            diff = diffs.tile([P, N_TILE], F32, name="diff")
            nc.vector.scalar_tensor_tensor(
                out=diff[:],
                in0=proto_sb[m][:, cols],
                scalar=minus_gs[:, m : m + 1],
                in1=acc[m, n][:],
                op0=MULT,
                op1=ADD,
            )
            half = SHOT // 2
            twice = diff[:].unsqueeze(1).to_broadcast([P, half, N_TILE])
            nc.scalar.activation(
                out=repeated[m][:, 0:half, cols],
                in_=twice,
                func=COPY,
                scale=two_over_denom[:, m : m + 1],
            )
            nc.vector.tensor_scalar_mul(
                out=repeated[m][:, half:SHOT, cols],
                in0=twice,
                scalar1=two_over_denom[:, m : m + 1],
            )

        def store_repeated(queue, m):
            queue.dma_start(
                out=out_dram[m].rearrange("p s d -> p (s d)"),
                in_=repeated[m][:].rearrange("p s d -> p (s d)"),
            )

        both = ("vector", "scalar")
        last = PASSES - 1
        early = FEATURE_TILES - 1
        for n in range(FEATURE_TILES):
            open_bank(0, n)
        regroup_q(0, 0, both)
        for c in range(last):
            regroup_q(c, 1, both)
            quantise_q(c, 0)
            regroup_q(c, 2, both)
            quantise_q(c, 1)
            regroup_q(c + 1, 0, both)
            if c == last - 1:
                one_over_denom = keep.tile([P, CLASS_TILES], F32, name="one_over_denom")
                nc.vector.reciprocal(out=one_over_denom[:], in_=denom_ps[:, 0:CLASS_TILES])
                two_over_denom = keep.tile([P, CLASS_TILES], F32, name="two_over_denom")
                nc.vector.tensor_scalar_mul(
                    out=two_over_denom[:], in0=one_over_denom[:], scalar1=2.0
                )
            quantise_q(c, 2)
        regroup_g(nc.vector.tensor_copy, 0, 0, 2)
        regroup_q(last, 1, both)
        quantise_g(0, 0, 2)
        sum_grad_out(0, 0, 2)
        for c in range(2):
            for n in range(early):
                multiply(c, 0, n)
        quantise_q(last, 0)
        regroup_q(last, 2, ("scalar",))
        regroup_g(nc.vector.tensor_copy, 0, 2, PASSES)
        quantise_q(last, 1)
        quantise_g(0, 2, PASSES)
        sum_grad_out(0, 2, PASSES)
        make_proto_factor(0)
        for n in range(early):
            multiply(2, 0, n)
            multiply(last, 0, n)
        for n in range(early):
            scale_proto(0, n)
            finish(0, n)
        store(nc.sync, 0, 0, early * N_TILE)

        gs_banks.append(psum_small.tile([P, 2, GS_COLS], F32, name="gs_odd", tag="denom_ps"))
        sum_grad_out(1, 0, PASSES)
        for c in range(last):
            multiply(c, 0, early)
        sum_grad_out(2, 0, PASSES)
        regroup_g(nc.scalar.copy, 1, 2, PASSES)
        scale_proto(0, early)
        regroup_g(nc.vector.tensor_copy, 1, 0, 2)
        regroup_q(last, 2, ("vector",))
        make_proto_factor(1)
        quantise_g(1, 0, PASSES)
        quantise_q(last, 2)
        for n in range(FEATURE_TILES):
            open_bank(1, n)
            scale_proto(1, n)
        regroup_g(nc.scalar.copy, 2, 2, PASSES)
        regroup_g(nc.scalar.copy, 3, 2, PASSES)
        for c in range(PASSES):
            multiply(c, 1, 0)
        multiply(last, 0, early)
        finish(1, 0)
        finish(0, early)
        store(nc.sync, 0, early * N_TILE, FEATURES)
        for c in range(PASSES):
            multiply(c, 1, 1)
        finish(1, 1)
        regroup_g(nc.vector.tensor_copy, 2, 0, 2)
        for c in range(PASSES):
            multiply(c, 1, 2)
        finish(1, 2)
        store(nc.scalar, 1, 0, FEATURES)
        quantise_g(2, 0, PASSES)
        regroup_g(nc.vector.tensor_copy, 3, 0, 2)
        make_minus_gs(2)
        quantise_g(3, 0, PASSES)

        for m in range(PLAIN_TILES, CLASS_TILES):
            repeated[m] = big.tile([P, SHOT, FEATURES], F32, name="repeated%d" % m, tag="big")
            for n in range(FEATURE_TILES):
                open_bank(m, n)
                for c in range(PASSES):
                    multiply(c, m, n)
                finish_repeated(m, n)
            store_repeated(nc.sync if m == PLAIN_TILES else nc.scalar, m)
            if m == PLAIN_TILES:
                sum_grad_out(3, 0, PASSES)
                make_minus_gs(3)
